import numpy as np
import ml_dtypes


def mxq(x, axis, fmt="e4m3"):
    dtype, down = {"e4m3": (ml_dtypes.float8_e4m3fn, 7), "e5m2": (ml_dtypes.float8_e5m2, 14)}[fmt]
    v = np.moveaxis(np.asarray(x, np.float32).astype(ml_dtypes.bfloat16).astype(np.float64), axis, -1)
    blocks = v.reshape(v.shape[:-1] + (-1, 32))
    amax = np.abs(blocks).max(-1, keepdims=True)
    byte = np.maximum(np.where(amax > 0, np.frexp(amax)[1] - 1 + 127, 0) - down, 1)
    scale = np.exp2(byte - 127.0)
    codes = (blocks / scale).astype(np.float32).astype(dtype).astype(np.float64)
    return np.moveaxis((codes * scale).reshape(v.shape), -1, axis)


WIDE = False


def mx_kscale(k):
    if not WIDE:
        return np.ones(k)
    levels = np.array([10, -10, 5, -5, 0])
    a = np.random.permutation(np.resize(levels, k // 512 * 4)).reshape(k // 512, 4)
    idx = np.arange(k)
    return np.exp2(a[idx // 512, idx % 128 // 32])


BF16 = ml_dtypes.bfloat16


def bf(x):
    return np.asarray(x, np.float32).astype(BF16)


def f64(x):
    return np.asarray(x).astype(np.float64)


E2M1 = np.array([0.0, 0.5, 1.0, 1.5, 2.0, 3.0, 4.0, 6.0, -0.0, -0.5, -1.0, -1.5, -2.0, -3.0, -4.0, -6.0])


def pack_weight(w, fmt):
    k, n = w.shape
    w = f64(bf(w)).reshape(k // 32, 32, n)
    amax = np.abs(w).max(1)
    if fmt == "e4m3":
        byte = np.frexp(amax)[1] - 1 + 127 - 7
    else:
        mant, ex = np.frexp(amax / 6.0)
        byte = np.where(mant > 0.5, ex, ex - 1) + 127
    byte = np.clip(np.where(amax > 0, byte, 1), 1, 254)
    scaled = (w * np.exp2(127.0 - byte)[:, None, :]).reshape(k, n).astype(np.float32)
    by_word = np.ascontiguousarray(scaled.reshape(k // 512, 128, 4, n).transpose(0, 1, 3, 2))
    if fmt == "e4m3":
        words = by_word.astype(ml_dtypes.float8_e4m3fn).view(np.uint8)
    else:
        c = by_word.astype(ml_dtypes.float4_e2m1fn).view(np.uint8) & 0xF
        words = c[..., 0::2] | (c[..., 1::2] << 4)
    return np.ascontiguousarray(words), np.ascontiguousarray(byte.astype(np.uint8).reshape(k // 512, 16, n))


def unpack_weight(words, scales, fmt):
    g, p, n, _ = words.shape
    if fmt == "e4m3":
        vals = np.ascontiguousarray(words).view(ml_dtypes.float8_e4m3fn).astype(np.float64)
    else:
        nib = np.empty((g, p, n, 4), np.uint8)
        nib[..., 0::2] = words & 0xF
        nib[..., 1::2] = words >> 4
        vals = E2M1[nib]
    vals = vals * np.repeat(np.exp2(scales.astype(np.float64) - 127.0), 8, axis=1)[..., None]
    return vals.transpose(0, 1, 3, 2).reshape(g * 512, n)

def pack4(w):
    words, scales = pack_weight(w, "e2m1")
    return words.reshape(words.shape[0], 128, -1), scales


def unpack4(words, scales):
    return unpack_weight(words.reshape(words.shape[0], 128, -1, 2), scales, "e2m1")


B, D_IN, H1, H2, H3, C = 1024, 2048, 2048, 2048, 1024, 1024
BN_EPS = 1e-5


def bn_relu(z, gamma, beta):
    m = z.mean(axis=0)
    v = z.var(axis=0)
    return np.maximum((z - m) * (1.0 / np.sqrt(v + BN_EPS)) * gamma + beta, 0.0)


def setup_inputs():
    t = mx_kscale(H3)
    c = 32.0 * np.exp2(-15.0 * np.random.random(H3))
    mu = 0.5 * np.random.standard_normal(H3)
    z2 = bf((np.random.standard_normal((B, H3)) + mu) * c)
    g2 = bf((1.0 + 0.1 * np.random.standard_normal(H3)) * t)
    beta2 = bf(0.2 * np.random.standard_normal(H3) * t)
    w3 = np.random.standard_normal((C, H3)) * 3.0 / np.sqrt(H3) / t
    words, scales = pack4(np.ascontiguousarray(w3.T))
    b3 = bf(0.5 * np.random.standard_normal(C))
    return {"z2": z2,
            "g2": g2,
            "beta2": beta2,
            "W3_words": words,
            "W3_scales": scales,
            "b3": b3}


def reference(z2, g2, beta2, W3_words, W3_scales, b3):
    h = bn_relu(f64(z2), f64(g2), f64(beta2))
    logits = (mxq(h, 1, "e4m3") @ unpack4(W3_words, W3_scales)) + f64(b3)
    s = logits - logits.max(axis=1, keepdims=True)
    return s - np.log(np.exp(s).sum(axis=1, keepdims=True))

@@ -1,0 +1,214 @@
+from contextlib import ExitStack
+
+import concourse.mybir as mybir
+from concourse.masks import make_identity
+
+F32 = mybir.dt.float32
+BF16 = mybir.dt.bfloat16
+U8 = mybir.dt.uint8
+U32 = mybir.dt.uint32
+I32 = mybir.dt.int32
+FP8X4 = mybir.dt.float8_e4m3fn_x4
+FP4X4 = mybir.dt.float4_e2m1fn_x4
+ALU = mybir.AluOpType
+ACT = mybir.ActivationFunctionType
+AXIS = mybir.AxisListType
+
+P = 128
+PACK = 4
+K_PASS = P * PACK
+BATCH = 1024
+FEATURES = 1024
+CLASSES = 1024
+PASSES = FEATURES // K_PASS
+PLANES = PASSES * PACK
+B_TILES = BATCH // P
+BANK = 512
+B_HALVES = BATCH // BANK
+TILES_PER_BANK = BANK // P
+N_HALVES = CLASSES // BANK
+STATS_MAX = 512
+STATS_CALLS = 2 * BATCH // STATS_MAX
+GROUP = 4
+BN_EPS = 1e-5
+
+FLOPS = 2 * BATCH * FEATURES * CLASSES
+
+
+def tile_binarymlp_pb_kernel(tc, z2, g2, beta2, W3_words, W3_scales, b3, out):
+    nc = tc.nc
+    with ExitStack() as ctx:
+        keep = ctx.enter_context(tc.tile_pool(name="keep", bufs=1))
+        scratch = ctx.enter_context(tc.tile_pool(name="scratch", bufs=2))
+        banks = ctx.enter_context(tc.psum_pool(name="banks", bufs=8))
+
+        z_rows = z2.rearrange("(p i) k -> p i k", i=B_TILES)
+        out_rows = out.rearrange("(p i) n -> p i n", i=B_TILES)
+
+        gain = keep.tile([P, PLANES], BF16)
+        beta = keep.tile([P, PLANES], BF16)
+        nc.scalar.dma_start(
+            out=gain[:].rearrange("p (g t) -> p g t", t=PACK),
+            in_=g2.rearrange("(g p t) -> p g t", p=P, t=PACK),
+        )
+        nc.scalar.dma_start(
+            out=beta[:].rearrange("p (g t) -> p g t", t=PACK),
+            in_=beta2.rearrange("(g p t) -> p g t", p=P, t=PACK),
+        )
+
+        z_sb = keep.tile([P, B_TILES, FEATURES], BF16)
+        for g in range(PASSES):
+            for first in range(0, B_TILES, 2):
+                tiles = slice(first, first + 2)
+                ks = slice(K_PASS * g, K_PASS * (g + 1))
+                nc.sync.dma_start(out=z_sb[:, tiles, ks], in_=z_rows[:, tiles, ks])
+
+        w_words = keep.tile([P, PASSES, 2 * CLASSES], U8, align_bytes=64)
+        for g in range(PASSES):
+            nc.sync.dma_start(out=w_words[:, g, :].bitcast(I32), in_=W3_words[g].bitcast(I32))
+
+        w_scales = keep.tile([P, PASSES, CLASSES], U8, align_bytes=64)
+        nc.vector.memset(w_scales[:].bitcast(I32), 0)
+        for quadrant in range(4):
+            nc.sync.dma_start(
+                out=w_scales[32 * quadrant : 32 * quadrant + 4, :, :].bitcast(I32),
+                in_=W3_scales[:, 4 * quadrant : 4 * quadrant + 4, :].rearrange("g r n -> r g n").bitcast(I32),
+            )
+
+        bias_rows = keep.tile([P, CLASSES], BF16)
+        nc.sync.dma_start(out=bias_rows[:], in_=b3.partition_broadcast(P))
+
+        identity = keep.tile([P, P], F32)
+        make_identity(nc, identity[:])
+
+        zT = {}
+        for g in range(PASSES):
+            for half in range(B_HALVES):
+                for u in range(2):
+                    zT[(g, u, half)] = banks.tile([P, BANK], F32, tag="bank", name="zT_%d_%d_%d" % (g, u, half))
+                    for slot in range(TILES_PER_BANK):
+                        words = z_sb[:, TILES_PER_BANK * half + slot, :].bitcast(F32)
+                        nc.tensor.transpose(
+                            zT[(g, u, half)][:, P * slot : P * (slot + 1)],
+                            words[:, 256 * g + u : 256 * (g + 1) : 2],
+                            identity[:],
+                        )
+
+        stats = keep.tile([P, PASSES * 2, STATS_CALLS, 6], F32)
+        mean_var = keep.tile([P, PLANES, 2], F32)
+        var_eps = keep.tile([P, PLANES], F32)
+        std = keep.tile([P, PLANES], F32)
+        rstd = keep.tile([P, PLANES], F32)
+        scale = keep.tile([P, PLANES], F32)
+        mean_scaled = keep.tile([P, PLANES], F32)
+        shift = keep.tile([P, PLANES], F32)
+        planes = keep.tile([P, PASSES, PACK, BATCH], BF16)
+        grouped = keep.tile([P, PASSES, BATCH, PACK], BF16, align_bytes=64)
+        h_codes = keep.tile([P, PASSES, BATCH], U32, align_bytes=64)
+        h_scales = keep.tile([P, PASSES, BATCH], U8, align_bytes=64)
+
+        for g in range(PASSES):
+            for u in range(2):
+                pair = 2 * g + u
+                js = slice(2 * pair, 2 * pair + 2)
+                for half in range(B_HALVES):
+                    values = zT[(g, u, half)][:].bitcast(BF16)
+                    for c in range(2 * BANK // STATS_MAX):
+                        nc.vector.bn_stats(
+                            out=stats[:, pair, 2 * half + c, :],
+                            in_=values[:, STATS_MAX * c : STATS_MAX * (c + 1)],
+                        )
+                for e in range(2):
+                    nc.vector.bn_aggr(out=mean_var[:, 2 * pair + e, :], in_=stats[:, pair, :, 3 * e : 3 * e + 3])
+                nc.vector.tensor_scalar_add(out=var_eps[:, js], in0=mean_var[:, js, 1], scalar1=BN_EPS)
+                nc.scalar.activation(out=std[:, js], in_=var_eps[:, js], func=ACT.Sqrt)
+                nc.vector.reciprocal(out=rstd[:, js], in_=std[:, js])
+                nc.vector.tensor_mul(out=scale[:, js], in0=gain[:, js], in1=rstd[:, js])
+                nc.vector.tensor_mul(out=mean_scaled[:, js], in0=mean_var[:, js, 0], in1=scale[:, js])
+                nc.vector.tensor_sub(out=shift[:, js], in0=beta[:, js], in1=mean_scaled[:, js])
+                for half in range(B_HALVES):
+                    values = zT[(g, u, half)][:].bitcast(BF16).rearrange("p (b e) -> p b e", e=2)
+                    for e in range(2):
+                        j = 2 * pair + e
+                        nc.scalar.activation(
+                            out=planes[:, g, 2 * u + e, BANK * half : BANK * (half + 1)],
+                            in_=values[:, :, e],
+                            func=ACT.Relu,
+                            bias=shift[:, j : j + 1],
+                            scale=scale[:, j : j + 1],
+                        )
+            for half in range(B_HALVES):
+                bs = slice(BANK * half, BANK * (half + 1))
+                if g < PASSES - 1:
+                    nc.gpsimd.tensor_scalar(
+                        out=grouped[:, g, bs, :],
+                        in0=planes[:, g, :, bs].rearrange("p t b -> p b t"),
+                        scalar1=1.0,
+                        scalar2=0.0,
+                        op0=ALU.mult,
+                        op1=ALU.add,
+                    )
+                else:
+                    nc.vector.tensor_copy(
+                        out=grouped[:, g, bs, :].rearrange("p (c i) t -> p c t i", i=4),
+                        in_=planes[:, g, :, bs].rearrange("p t (c i) -> p c t i", i=4),
+                    )
+        for g in range(PASSES):
+            for half in range(B_HALVES):
+                bs = slice(BANK * half, BANK * (half + 1))
+                nc.vector.quantize_mx(
+                    out=h_codes[:, g, bs].bitcast(FP8X4),
+                    scales=h_scales[:, g, bs],
+                    in_=grouped[:, g, bs, :].rearrange("p b t -> p (b t)"),
+                )
+
+        logits = keep.tile([P, B_TILES, CLASSES], F32)
+        neg_max = keep.tile([P, B_TILES], F32)
+        exp_sum = keep.tile([P, B_TILES], F32)
+        log_sum = keep.tile([P, B_TILES], F32)
+        neg_lse = keep.tile([P, B_TILES], F32)
+
+        for i in range(B_TILES):
+            bs = slice(P * i, P * (i + 1))
+            acc = [banks.tile([P, BANK], F32, tag="bank", name="acc_%d_%d" % (i, nh)) for nh in range(N_HALVES)]
+            for g in range(PASSES):
+                for nh in range(N_HALVES):
+                    nc.tensor.matmul_mx(
+                        out=acc[nh][:],
+                        lhsT=h_codes[:, g, bs].bitcast(FP8X4),
+                        lhsT_scale=h_scales[:, g, bs],
+                        rhs=w_words[:, g, 2 * BANK * nh : 2 * BANK * (nh + 1)].bitcast(FP4X4),
+                        rhs_scale=w_scales[:, g, BANK * nh : BANK * (nh + 1)],
+                        start=(g == 0),
+                        stop=(g == PASSES - 1),
+                    )
+            for nh in range(N_HALVES):
+                ns = slice(BANK * nh, BANK * (nh + 1))
+                nc.vector.tensor_add(out=logits[:, i, ns], in0=acc[nh][:], in1=bias_rows[:, ns])
+            nc.vector.tensor_reduce(out=neg_max[:, i : i + 1], in_=logits[:, i, :], axis=AXIS.X, op=ALU.max, negate=True)
+            exps = scratch.tile([P, CLASSES], BF16)
+            nc.scalar.activation(
+                out=exps[:],
+                in_=logits[:, i, :],
+                func=ACT.Exp,
+                bias=neg_max[:, i : i + 1],
+                scale=1.0,
+                accum_out=exp_sum[:, i : i + 1],
+            )
+            if i % GROUP == GROUP - 1:
+                group = slice(i + 1 - GROUP, i + 1)
+                nc.scalar.activation(out=log_sum[:, group], in_=exp_sum[:, group], func=ACT.Ln)
+                nc.vector.tensor_sub(out=neg_lse[:, group], in0=neg_max[:, group], in1=log_sum[:, group])
+                for k in range(i + 1 - GROUP, i + 1):
+                    if i < B_TILES - 1:
+                        nc.gpsimd.tensor_scalar(
+                            out=logits[:, k, :],
+                            in0=logits[:, k, :],
+                            scalar1=1.0,
+                            scalar2=neg_lse[:, k : k + 1],
+                            op0=ALU.mult,
+                            op1=ALU.add,
+                        )
+                    else:
+                        nc.vector.tensor_scalar_add(out=logits[:, k, :], in0=logits[:, k, :], scalar1=neg_lse[:, k : k + 1])
+                    nc.sync.dma_start(out=out_rows[:, k, :], in_=logits[:, k, :])

@@ -47,14 +47,6 @@ def tile_binarymlp_pb_kernel(tc, z2, g2, beta2, W3_words, W3_scales, b3, out):
 
         gain = keep.tile([P, PLANES], BF16)
         beta = keep.tile([P, PLANES], BF16)
-        nc.scalar.dma_start(
-            out=gain[:].rearrange("p (g t) -> p g t", t=PACK),
-            in_=g2.rearrange("(g p t) -> p g t", p=P, t=PACK),
-        )
-        nc.scalar.dma_start(
-            out=beta[:].rearrange("p (g t) -> p g t", t=PACK),
-            in_=beta2.rearrange("(g p t) -> p g t", p=P, t=PACK),
-        )
 
         z_sb = keep.tile([P, B_TILES, FEATURES], BF16)
         for g in range(PASSES):
@@ -62,6 +54,15 @@ def tile_binarymlp_pb_kernel(tc, z2, g2, beta2, W3_words, W3_scales, b3, out):
                 tiles = slice(first, first + 2)
                 ks = slice(K_PASS * g, K_PASS * (g + 1))
                 nc.sync.dma_start(out=z_sb[:, tiles, ks], in_=z_rows[:, tiles, ks])
+            if g == 0:
+                nc.sync.dma_start(
+                    out=gain[:].rearrange("p (g t) -> p g t", t=PACK),
+                    in_=g2.rearrange("(g p t) -> p g t", p=P, t=PACK),
+                )
+                nc.sync.dma_start(
+                    out=beta[:].rearrange("p (g t) -> p g t", t=PACK),
+                    in_=beta2.rearrange("(g p t) -> p g t", p=P, t=PACK),
+                )
 
         w_words = keep.tile([P, PASSES, 2 * CLASSES], U8, align_bytes=64)
         for g in range(PASSES):
@@ -80,6 +81,8 @@ def tile_binarymlp_pb_kernel(tc, z2, g2, beta2, W3_words, W3_scales, b3, out):
 
         identity = keep.tile([P, P], F32)
         make_identity(nc, identity[:])
+        minus_half = keep.tile([P, PLANES], F32)
+        nc.gpsimd.memset(minus_half[:], -0.5)
 
         zT = {}
         for g in range(PASSES):
@@ -97,7 +100,6 @@ def tile_binarymlp_pb_kernel(tc, z2, g2, beta2, W3_words, W3_scales, b3, out):
         stats = keep.tile([P, PASSES * 2, STATS_CALLS, 6], F32)
         mean_var = keep.tile([P, PLANES, 2], F32)
         var_eps = keep.tile([P, PLANES], F32)
-        std = keep.tile([P, PLANES], F32)
         rstd = keep.tile([P, PLANES], F32)
         scale = keep.tile([P, PLANES], F32)
         mean_scaled = keep.tile([P, PLANES], F32)
@@ -120,12 +122,11 @@ def tile_binarymlp_pb_kernel(tc, z2, g2, beta2, W3_words, W3_scales, b3, out):
                         )
                 for e in range(2):
                     nc.vector.bn_aggr(out=mean_var[:, 2 * pair + e, :], in_=stats[:, pair, :, 3 * e : 3 * e + 3])
-                nc.vector.tensor_scalar_add(out=var_eps[:, js], in0=mean_var[:, js, 1], scalar1=BN_EPS)
-                nc.scalar.activation(out=std[:, js], in_=var_eps[:, js], func=ACT.Sqrt)
-                nc.vector.reciprocal(out=rstd[:, js], in_=std[:, js])
-                nc.vector.tensor_mul(out=scale[:, js], in0=gain[:, js], in1=rstd[:, js])
-                nc.vector.tensor_mul(out=mean_scaled[:, js], in0=mean_var[:, js, 0], in1=scale[:, js])
-                nc.vector.tensor_sub(out=shift[:, js], in0=beta[:, js], in1=mean_scaled[:, js])
+                nc.gpsimd.tensor_scalar_add(out=var_eps[:, js], in0=mean_var[:, js, 1], scalar1=BN_EPS)
+                nc.gpsimd.tensor_tensor(out=rstd[:, js], in0=var_eps[:, js], in1=minus_half[:, js], op=ALU.pow)
+                nc.gpsimd.tensor_mul(out=scale[:, js], in0=gain[:, js], in1=rstd[:, js])
+                nc.gpsimd.tensor_mul(out=mean_scaled[:, js], in0=mean_var[:, js, 0], in1=scale[:, js])
+                nc.gpsimd.tensor_sub(out=shift[:, js], in0=beta[:, js], in1=mean_scaled[:, js])
                 for half in range(B_HALVES):
                     values = zT[(g, u, half)][:].bitcast(BF16).rearrange("p (b e) -> p b e", e=2)
                     for e in range(2):
@@ -137,23 +138,13 @@ def tile_binarymlp_pb_kernel(tc, z2, g2, beta2, W3_words, W3_scales, b3, out):
                             bias=shift[:, j : j + 1],
                             scale=scale[:, j : j + 1],
                         )
+        for g in range(PASSES):
             for half in range(B_HALVES):
                 bs = slice(BANK * half, BANK * (half + 1))
-                if g < PASSES - 1:
-                    nc.gpsimd.tensor_scalar(
-                        out=grouped[:, g, bs, :],
-                        in0=planes[:, g, :, bs].rearrange("p t b -> p b t"),
-                        scalar1=1.0,
-                        scalar2=0.0,
-                        op0=ALU.mult,
-                        op1=ALU.add,
-                    )
-                else:
-                    nc.vector.tensor_copy(
-                        out=grouped[:, g, bs, :].rearrange("p (c i) t -> p c t i", i=4),
-                        in_=planes[:, g, :, bs].rearrange("p t (c i) -> p c t i", i=4),
-                    )
-        for g in range(PASSES):
+                nc.vector.tensor_copy(
+                    out=grouped[:, g, bs, :].rearrange("p (c i) t -> p c t i", i=4),
+                    in_=planes[:, g, :, bs].rearrange("p t (c i) -> p c t i", i=4),
+                )
             for half in range(B_HALVES):
                 bs = slice(BANK * half, BANK * (half + 1))
                 nc.vector.quantize_mx(

@@ -22,13 +22,14 @@ FEATURES = 1024
 CLASSES = 1024
 PASSES = FEATURES // K_PASS
 PLANES = PASSES * PACK
+PAIRS = PLANES // 2
 B_TILES = BATCH // P
 BANK = 512
 B_HALVES = BATCH // BANK
 TILES_PER_BANK = BANK // P
 N_HALVES = CLASSES // BANK
 STATS_MAX = 512
-STATS_CALLS = 2 * BATCH // STATS_MAX
+STATS_PER_BANK = 2 * BANK // STATS_MAX
 GROUP = 4
 BN_EPS = 1e-5
 
@@ -38,9 +39,15 @@ FLOPS = 2 * BATCH * FEATURES * CLASSES
 def tile_binarymlp_pb_kernel(tc, z2, g2, beta2, W3_words, W3_scales, b3, out):
     nc = tc.nc
     with ExitStack() as ctx:
+        ctx.enter_context(tc.manual_schedule())
         keep = ctx.enter_context(tc.tile_pool(name="keep", bufs=1))
         scratch = ctx.enter_context(tc.tile_pool(name="scratch", bufs=2))
         banks = ctx.enter_context(tc.psum_pool(name="banks", bufs=8))
+
+        identity = keep.tile([P, P], F32)
+        make_identity(nc, identity[:])
+        minus_half = keep.tile([P, PLANES], F32)
+        nc.gpsimd.memset(minus_half[:], -0.5)
 
         z_rows = z2.rearrange("(p i) k -> p i k", i=B_TILES)
         out_rows = out.rearrange("(p i) n -> p i n", i=B_TILES)
@@ -50,8 +57,8 @@ def tile_binarymlp_pb_kernel(tc, z2, g2, beta2, W3_words, W3_scales, b3, out):
 
         z_sb = keep.tile([P, B_TILES, FEATURES], BF16)
         for g in range(PASSES):
-            for first in range(0, B_TILES, 2):
-                tiles = slice(first, first + 2)
+            for half in range(B_HALVES):
+                tiles = slice(TILES_PER_BANK * half, TILES_PER_BANK * (half + 1))
                 ks = slice(K_PASS * g, K_PASS * (g + 1))
                 nc.sync.dma_start(out=z_sb[:, tiles, ks], in_=z_rows[:, tiles, ks])
             if g == 0:
@@ -79,25 +86,21 @@ def tile_binarymlp_pb_kernel(tc, z2, g2, beta2, W3_words, W3_scales, b3, out):
         bias_rows = keep.tile([P, CLASSES], BF16)
         nc.sync.dma_start(out=bias_rows[:], in_=b3.partition_broadcast(P))
 
-        identity = keep.tile([P, P], F32)
-        make_identity(nc, identity[:])
-        minus_half = keep.tile([P, PLANES], F32)
-        nc.gpsimd.memset(minus_half[:], -0.5)
-
         zT = {}
         for g in range(PASSES):
             for half in range(B_HALVES):
                 for u in range(2):
-                    zT[(g, u, half)] = banks.tile([P, BANK], F32, tag="bank", name="zT_%d_%d_%d" % (g, u, half))
+                    bank = banks.tile([P, BANK], F32, tag="bank", name="zT_%d_%d_%d" % (g, u, half))
+                    zT[(2 * g + u, half)] = bank
                     for slot in range(TILES_PER_BANK):
                         words = z_sb[:, TILES_PER_BANK * half + slot, :].bitcast(F32)
                         nc.tensor.transpose(
-                            zT[(g, u, half)][:, P * slot : P * (slot + 1)],
+                            bank[:, P * slot : P * (slot + 1)],
                             words[:, 256 * g + u : 256 * (g + 1) : 2],
                             identity[:],
                         )
 
-        stats = keep.tile([P, PASSES * 2, STATS_CALLS, 6], F32)
+        stats = keep.tile([P, PAIRS, B_HALVES * STATS_PER_BANK, 6], F32)
         mean_var = keep.tile([P, PLANES, 2], F32)
         var_eps = keep.tile([P, PLANES], F32)
         rstd = keep.tile([P, PLANES], F32)
@@ -105,39 +108,44 @@ def tile_binarymlp_pb_kernel(tc, z2, g2, beta2, W3_words, W3_scales, b3, out):
         mean_scaled = keep.tile([P, PLANES], F32)
         shift = keep.tile([P, PLANES], F32)
         planes = keep.tile([P, PASSES, PACK, BATCH], BF16)
+
+        def statistics(pair):
+            js = slice(2 * pair, 2 * pair + 2)
+            for half in range(B_HALVES):
+                values = zT[(pair, half)][:].bitcast(BF16)
+                for c in range(STATS_PER_BANK):
+                    nc.vector.bn_stats(
+                        out=stats[:, pair, STATS_PER_BANK * half + c, :],
+                        in_=values[:, STATS_MAX * c : STATS_MAX * (c + 1)],
+                    )
+            for e in range(2):
+                nc.vector.bn_aggr(out=mean_var[:, 2 * pair + e, :], in_=stats[:, pair, :, 3 * e : 3 * e + 3])
+            nc.gpsimd.tensor_scalar_add(out=var_eps[:, js], in0=mean_var[:, js, 1], scalar1=BN_EPS)
+            nc.gpsimd.tensor_tensor(out=rstd[:, js], in0=var_eps[:, js], in1=minus_half[:, js], op=ALU.pow)
+            nc.gpsimd.tensor_mul(out=scale[:, js], in0=gain[:, js], in1=rstd[:, js])
+            nc.gpsimd.tensor_mul(out=mean_scaled[:, js], in0=mean_var[:, js, 0], in1=scale[:, js])
+            nc.gpsimd.tensor_sub(out=shift[:, js], in0=beta[:, js], in1=mean_scaled[:, js])
+
+        def norm_relu(pair):
+            for half in range(B_HALVES):
+                values = zT[(pair, half)][:].bitcast(BF16).rearrange("p (b e) -> p b e", e=2)
+                for e in range(2):
+                    j = 2 * pair + e
+                    nc.scalar.activation(
+                        out=planes[:, j // PACK, j % PACK, BANK * half : BANK * (half + 1)],
+                        in_=values[:, :, e],
+                        func=ACT.Relu,
+                        bias=shift[:, j : j + 1],
+                        scale=scale[:, j : j + 1],
+                    )
+
+        for pair in range(PAIRS):
+            statistics(pair)
+            norm_relu(pair)
+
         grouped = keep.tile([P, PASSES, BATCH, PACK], BF16, align_bytes=64)
         h_codes = keep.tile([P, PASSES, BATCH], U32, align_bytes=64)
         h_scales = keep.tile([P, PASSES, BATCH], U8, align_bytes=64)
-
-        for g in range(PASSES):
-            for u in range(2):
-                pair = 2 * g + u
-                js = slice(2 * pair, 2 * pair + 2)
-                for half in range(B_HALVES):
-                    values = zT[(g, u, half)][:].bitcast(BF16)
-                    for c in range(2 * BANK // STATS_MAX):
-                        nc.vector.bn_stats(
-                            out=stats[:, pair, 2 * half + c, :],
-                            in_=values[:, STATS_MAX * c : STATS_MAX * (c + 1)],
-                        )
-                for e in range(2):
-                    nc.vector.bn_aggr(out=mean_var[:, 2 * pair + e, :], in_=stats[:, pair, :, 3 * e : 3 * e + 3])
-                nc.gpsimd.tensor_scalar_add(out=var_eps[:, js], in0=mean_var[:, js, 1], scalar1=BN_EPS)
-                nc.gpsimd.tensor_tensor(out=rstd[:, js], in0=var_eps[:, js], in1=minus_half[:, js], op=ALU.pow)
-                nc.gpsimd.tensor_mul(out=scale[:, js], in0=gain[:, js], in1=rstd[:, js])
-                nc.gpsimd.tensor_mul(out=mean_scaled[:, js], in0=mean_var[:, js, 0], in1=scale[:, js])
-                nc.gpsimd.tensor_sub(out=shift[:, js], in0=beta[:, js], in1=mean_scaled[:, js])
-                for half in range(B_HALVES):
-                    values = zT[(g, u, half)][:].bitcast(BF16).rearrange("p (b e) -> p b e", e=2)
-                    for e in range(2):
-                        j = 2 * pair + e
-                        nc.scalar.activation(
-                            out=planes[:, g, 2 * u + e, BANK * half : BANK * (half + 1)],
-                            in_=values[:, :, e],
-                            func=ACT.Relu,
-                            bias=shift[:, j : j + 1],
-                            scale=scale[:, j : j + 1],
-                        )
         for g in range(PASSES):
             for half in range(B_HALVES):
                 bs = slice(BANK * half, BANK * (half + 1))
@@ -157,9 +165,8 @@ def tile_binarymlp_pb_kernel(tc, z2, g2, beta2, W3_words, W3_scales, b3, out):
         neg_max = keep.tile([P, B_TILES], F32)
         exp_sum = keep.tile([P, B_TILES], F32)
         log_sum = keep.tile([P, B_TILES], F32)
-        neg_lse = keep.tile([P, B_TILES], F32)
 
-        for i in range(B_TILES):
+        def biased_logits(i):
             bs = slice(P * i, P * (i + 1))
             acc = [banks.tile([P, BANK], F32, tag="bank", name="acc_%d_%d" % (i, nh)) for nh in range(N_HALVES)]
             for g in range(PASSES):
@@ -176,6 +183,8 @@ def tile_binarymlp_pb_kernel(tc, z2, g2, beta2, W3_words, W3_scales, b3, out):
             for nh in range(N_HALVES):
                 ns = slice(BANK * nh, BANK * (nh + 1))
                 nc.vector.tensor_add(out=logits[:, i, ns], in0=acc[nh][:], in1=bias_rows[:, ns])
+
+        def max_and_exp_sum(i):
             nc.vector.tensor_reduce(out=neg_max[:, i : i + 1], in_=logits[:, i, :], axis=AXIS.X, op=ALU.max, negate=True)
             exps = scratch.tile([P, CLASSES], BF16)
             nc.scalar.activation(
@@ -186,20 +195,28 @@ def tile_binarymlp_pb_kernel(tc, z2, g2, beta2, W3_words, W3_scales, b3, out):
                 scale=1.0,
                 accum_out=exp_sum[:, i : i + 1],
             )
-            if i % GROUP == GROUP - 1:
-                group = slice(i + 1 - GROUP, i + 1)
-                nc.scalar.activation(out=log_sum[:, group], in_=exp_sum[:, group], func=ACT.Ln)
-                nc.vector.tensor_sub(out=neg_lse[:, group], in0=neg_max[:, group], in1=log_sum[:, group])
-                for k in range(i + 1 - GROUP, i + 1):
-                    if i < B_TILES - 1:
-                        nc.gpsimd.tensor_scalar(
-                            out=logits[:, k, :],
-                            in0=logits[:, k, :],
-                            scalar1=1.0,
-                            scalar2=neg_lse[:, k : k + 1],
-                            op0=ALU.mult,
-                            op1=ALU.add,
-                        )
-                    else:
-                        nc.vector.tensor_scalar_add(out=logits[:, k, :], in0=logits[:, k, :], scalar1=neg_lse[:, k : k + 1])
-                    nc.sync.dma_start(out=out_rows[:, k, :], in_=logits[:, k, :])
+
+        def finish(first, engine):
+            group = slice(first, first + GROUP)
+            nc.scalar.activation(out=log_sum[:, group], in_=exp_sum[:, group], func=ACT.Ln)
+            neg_lse = keep.tile([P, GROUP], F32, name="neg_lse_%d" % first)
+            engine.tensor_sub(out=neg_lse[:], in0=neg_max[:, group], in1=log_sum[:, group])
+            for i in range(first, first + GROUP):
+                engine.tensor_scalar(
+                    out=logits[:, i, :],
+                    in0=logits[:, i, :],
+                    scalar1=1.0,
+                    scalar2=neg_lse[:, i - first : i - first + 1],
+                    op0=ALU.mult,
+                    op1=ALU.add,
+                )
+                nc.sync.dma_start(out=out_rows[:, i, :], in_=logits[:, i, :])
+
+        biased_logits(0)
+        for i in range(1, B_TILES):
+            biased_logits(i)
+            max_and_exp_sum(i - 1)
+            if i % GROUP == 0:
+                finish(i - GROUP, nc.gpsimd)
+        max_and_exp_sum(B_TILES - 1)
+        finish(B_TILES - GROUP, nc.vector)

@@ -55,12 +55,12 @@ def tile_binarymlp_pb_kernel(tc, z2, g2, beta2, W3_words, W3_scales, b3, out):
         gain = keep.tile([P, PLANES], BF16)
         beta = keep.tile([P, PLANES], BF16)
 
-        z_sb = keep.tile([P, B_TILES, FEATURES], BF16)
+        z_sb = [keep.tile([P, B_TILES, K_PASS], BF16, name="z_sb_%d" % g) for g in range(PASSES)]
         for g in range(PASSES):
             for half in range(B_HALVES):
                 tiles = slice(TILES_PER_BANK * half, TILES_PER_BANK * (half + 1))
                 ks = slice(K_PASS * g, K_PASS * (g + 1))
-                nc.sync.dma_start(out=z_sb[:, tiles, ks], in_=z_rows[:, tiles, ks])
+                nc.sync.dma_start(out=z_sb[g][:, tiles, :], in_=z_rows[:, tiles, ks])
             if g == 0:
                 nc.sync.dma_start(
                     out=gain[:].rearrange("p (g t) -> p g t", t=PACK),
@@ -88,17 +88,13 @@ def tile_binarymlp_pb_kernel(tc, z2, g2, beta2, W3_words, W3_scales, b3, out):
 
         zT = {}
         for g in range(PASSES):
-            for half in range(B_HALVES):
-                for u in range(2):
+            for u in range(2):
+                for half in range(B_HALVES):
                     bank = banks.tile([P, BANK], F32, tag="bank", name="zT_%d_%d_%d" % (g, u, half))
                     zT[(2 * g + u, half)] = bank
                     for slot in range(TILES_PER_BANK):
-                        words = z_sb[:, TILES_PER_BANK * half + slot, :].bitcast(F32)
-                        nc.tensor.transpose(
-                            bank[:, P * slot : P * (slot + 1)],
-                            words[:, 256 * g + u : 256 * (g + 1) : 2],
-                            identity[:],
-                        )
+                        words = z_sb[g][:, TILES_PER_BANK * half + slot, :].bitcast(F32)
+                        nc.tensor.transpose(bank[:, P * slot : P * (slot + 1)], words[:, u::2], identity[:])
 
         stats = keep.tile([P, PAIRS, B_HALVES * STATS_PER_BANK, 6], F32)
         mean_var = keep.tile([P, PLANES, 2], F32)
@@ -107,7 +103,7 @@ def tile_binarymlp_pb_kernel(tc, z2, g2, beta2, W3_words, W3_scales, b3, out):
         scale = keep.tile([P, PLANES], F32)
         mean_scaled = keep.tile([P, PLANES], F32)
         shift = keep.tile([P, PLANES], F32)
-        planes = keep.tile([P, PASSES, PACK, BATCH], BF16)
+        planes = keep.tile([P, PASSES, B_HALVES, PACK, BANK], BF16)
 
         def statistics(pair):
             js = slice(2 * pair, 2 * pair + 2)
@@ -132,7 +128,7 @@ def tile_binarymlp_pb_kernel(tc, z2, g2, beta2, W3_words, W3_scales, b3, out):
                 for e in range(2):
                     j = 2 * pair + e
                     nc.scalar.activation(
-                        out=planes[:, j // PACK, j % PACK, BANK * half : BANK * (half + 1)],
+                        out=planes[:, j // PACK, half, j % PACK, :],
                         in_=values[:, :, e],
                         func=ACT.Relu,
                         bias=shift[:, j : j + 1],
@@ -151,7 +147,7 @@ def tile_binarymlp_pb_kernel(tc, z2, g2, beta2, W3_words, W3_scales, b3, out):
                 bs = slice(BANK * half, BANK * (half + 1))
                 nc.vector.tensor_copy(
                     out=grouped[:, g, bs, :].rearrange("p (c i) t -> p c t i", i=4),
-                    in_=planes[:, g, :, bs].rearrange("p t (c i) -> p c t i", i=4),
+                    in_=planes[:, g, half, :, :].rearrange("p t (c i) -> p c t i", i=4),
                 )
             for half in range(B_HALVES):
                 bs = slice(BANK * half, BANK * (half + 1))

@@ -162,23 +162,30 @@ def tile_binarymlp_pb_kernel(tc, z2, g2, beta2, W3_words, W3_scales, b3, out):
         exp_sum = keep.tile([P, B_TILES], F32)
         log_sum = keep.tile([P, B_TILES], F32)
 
-        def biased_logits(i):
-            bs = slice(P * i, P * (i + 1))
-            acc = [banks.tile([P, BANK], F32, tag="bank", name="acc_%d_%d" % (i, nh)) for nh in range(N_HALVES)]
-            for g in range(PASSES):
+        acc = {}
+
+        def matmuls(first):
+            tiles = range(first, first + TILES_PER_BANK)
+            for i in tiles:
                 for nh in range(N_HALVES):
-                    nc.tensor.matmul_mx(
-                        out=acc[nh][:],
-                        lhsT=h_codes[:, g, bs].bitcast(FP8X4),
-                        lhsT_scale=h_scales[:, g, bs],
-                        rhs=w_words[:, g, 2 * BANK * nh : 2 * BANK * (nh + 1)].bitcast(FP4X4),
-                        rhs_scale=w_scales[:, g, BANK * nh : BANK * (nh + 1)],
-                        start=(g == 0),
-                        stop=(g == PASSES - 1),
-                    )
+                    acc[(i, nh)] = banks.tile([P, BANK], F32, tag="bank", name="acc_%d_%d" % (i, nh))
+            for g in range(PASSES):
+                for i in tiles:
+                    for nh in range(N_HALVES):
+                        nc.tensor.matmul_mx(
+                            out=acc[(i, nh)][:],
+                            lhsT=h_codes[:, g, P * i : P * (i + 1)].bitcast(FP8X4),
+                            lhsT_scale=h_scales[:, g, P * i : P * (i + 1)],
+                            rhs=w_words[:, g, 2 * BANK * nh : 2 * BANK * (nh + 1)].bitcast(FP4X4),
+                            rhs_scale=w_scales[:, g, BANK * nh : BANK * (nh + 1)],
+                            start=(g == 0),
+                            stop=(g == PASSES - 1),
+                        )
+
+        def add_bias(i):
             for nh in range(N_HALVES):
                 ns = slice(BANK * nh, BANK * (nh + 1))
-                nc.vector.tensor_add(out=logits[:, i, ns], in0=acc[nh][:], in1=bias_rows[:, ns])
+                nc.vector.tensor_add(out=logits[:, i, ns], in0=acc[(i, nh)][:], in1=bias_rows[:, ns])
 
         def max_and_exp_sum(i):
             nc.vector.tensor_reduce(out=neg_max[:, i : i + 1], in_=logits[:, i, :], axis=AXIS.X, op=ALU.max, negate=True)
@@ -208,11 +215,13 @@ def tile_binarymlp_pb_kernel(tc, z2, g2, beta2, W3_words, W3_scales, b3, out):
                 )
                 nc.sync.dma_start(out=out_rows[:, i, :], in_=logits[:, i, :])
 
-        biased_logits(0)
-        for i in range(1, B_TILES):
-            biased_logits(i)
-            max_and_exp_sum(i - 1)
-            if i % GROUP == 0:
-                finish(i - GROUP, nc.gpsimd)
+        for i in range(B_TILES):
+            if i % TILES_PER_BANK == 0:
+                matmuls(i)
+            add_bias(i)
+            if i > 0:
+                max_and_exp_sum(i - 1)
+            if i == GROUP:
+                finish(0, nc.gpsimd)
         max_and_exp_sum(B_TILES - 1)
-        finish(B_TILES - GROUP, nc.vector)
+        finish(GROUP, nc.vector)

@@ -57,10 +57,9 @@ def tile_binarymlp_pb_kernel(tc, z2, g2, beta2, W3_words, W3_scales, b3, out):
 
         z_sb = [keep.tile([P, B_TILES, K_PASS], BF16, name="z_sb_%d" % g) for g in range(PASSES)]
         for g in range(PASSES):
-            for half in range(B_HALVES):
-                tiles = slice(TILES_PER_BANK * half, TILES_PER_BANK * (half + 1))
+            for first in range(0, B_TILES, 2):
                 ks = slice(K_PASS * g, K_PASS * (g + 1))
-                nc.sync.dma_start(out=z_sb[g][:, tiles, :], in_=z_rows[:, tiles, ks])
+                nc.sync.dma_start(out=z_sb[g][:, first : first + 2, :], in_=z_rows[:, first : first + 2, ks])
             if g == 0:
                 nc.sync.dma_start(
                     out=gain[:].rearrange("p (g t) -> p g t", t=PACK),

@@ -214,13 +214,24 @@ def tile_binarymlp_pb_kernel(tc, z2, g2, beta2, W3_words, W3_scales, b3, out):
                 )
                 nc.sync.dma_start(out=out_rows[:, i, :], in_=logits[:, i, :])
 
-        for i in range(B_TILES):
-            if i % TILES_PER_BANK == 0:
-                matmuls(i)
+        def add_bias_beside_vector(i):
+            for nh in range(N_HALVES):
+                ns = slice(BANK * nh, BANK * (nh + 1))
+                nc.scalar.copy(out=logits[:, i, ns], in_=acc[(i, nh)][:])
+            nc.gpsimd.tensor_add(out=logits[:, i, :], in0=logits[:, i, :], in1=bias_rows[:])
+
+        matmuls(0)
+        add_bias(0)
+        add_bias_beside_vector(1)
+        add_bias(2)
+        add_bias_beside_vector(3)
+        matmuls(GROUP)
+        for i in range(GROUP):
+            max_and_exp_sum(i)
+        add_bias(GROUP)
+        finish(0, nc.gpsimd)
+        for i in range(GROUP + 1, B_TILES):
             add_bias(i)
-            if i > 0:
-                max_and_exp_sum(i - 1)
-            if i == GROUP:
-                finish(0, nc.gpsimd)
+            max_and_exp_sum(i - 1)
         max_and_exp_sum(B_TILES - 1)
         finish(GROUP, nc.vector)

@@ -46,8 +46,6 @@ def tile_binarymlp_pb_kernel(tc, z2, g2, beta2, W3_words, W3_scales, b3, out):
 
         identity = keep.tile([P, P], F32)
         make_identity(nc, identity[:])
-        minus_half = keep.tile([P, PLANES], F32)
-        nc.gpsimd.memset(minus_half[:], -0.5)
 
         z_rows = z2.rearrange("(p i) k -> p i k", i=B_TILES)
         out_rows = out.rearrange("(p i) n -> p i n", i=B_TILES)
@@ -97,10 +95,11 @@ def tile_binarymlp_pb_kernel(tc, z2, g2, beta2, W3_words, W3_scales, b3, out):
 
         stats = keep.tile([P, PAIRS, B_HALVES * STATS_PER_BANK, 6], F32)
         mean_var = keep.tile([P, PLANES, 2], F32)
-        var_eps = keep.tile([P, PLANES], F32)
+        neg_mean = keep.tile([P, PLANES], F32)
+        gain_f32 = keep.tile([P, PLANES], F32)
+        nc.gpsimd.tensor_copy(out=gain_f32[:], in_=gain[:])
         rstd = keep.tile([P, PLANES], F32)
         scale = keep.tile([P, PLANES], F32)
-        mean_scaled = keep.tile([P, PLANES], F32)
         shift = keep.tile([P, PLANES], F32)
         planes = keep.tile([P, PASSES, B_HALVES, PACK, BANK], BF16)
 
@@ -115,11 +114,18 @@ def tile_binarymlp_pb_kernel(tc, z2, g2, beta2, W3_words, W3_scales, b3, out):
                     )
             for e in range(2):
                 nc.vector.bn_aggr(out=mean_var[:, 2 * pair + e, :], in_=stats[:, pair, :, 3 * e : 3 * e + 3])
-            nc.gpsimd.tensor_scalar_add(out=var_eps[:, js], in0=mean_var[:, js, 1], scalar1=BN_EPS)
-            nc.gpsimd.tensor_tensor(out=rstd[:, js], in0=var_eps[:, js], in1=minus_half[:, js], op=ALU.pow)
-            nc.gpsimd.tensor_mul(out=scale[:, js], in0=gain[:, js], in1=rstd[:, js])
-            nc.gpsimd.tensor_mul(out=mean_scaled[:, js], in0=mean_var[:, js, 0], in1=scale[:, js])
-            nc.gpsimd.tensor_sub(out=shift[:, js], in0=beta[:, js], in1=mean_scaled[:, js])
+            nc.scalar.activation(out=rstd[:, js], in_=mean_var[:, js, 1], func=ACT.Abs_reciprocal_sqrt, bias=BN_EPS, scale=1.0)
+            nc.scalar.activation(out=neg_mean[:, js], in_=mean_var[:, js, 0], func=ACT.Copy, scale=-1.0)
+            for j in range(2 * pair, 2 * pair + 2):
+                nc.scalar.activation(out=scale[:, j : j + 1], in_=rstd[:, j : j + 1], func=ACT.Copy, scale=gain_f32[:, j : j + 1])
+            for j in range(2 * pair, 2 * pair + 2):
+                nc.scalar.activation(
+                    out=shift[:, j : j + 1],
+                    in_=scale[:, j : j + 1],
+                    func=ACT.Identity,
+                    bias=beta[:, j : j + 1],
+                    scale=neg_mean[:, j : j + 1],
+                )
 
         def norm_relu(pair):
             for half in range(B_HALVES):
@@ -137,6 +143,8 @@ def tile_binarymlp_pb_kernel(tc, z2, g2, beta2, W3_words, W3_scales, b3, out):
         for pair in range(PAIRS):
             statistics(pair)
             norm_relu(pair)
+        warm = keep.tile([P, 1], F32)
+        nc.scalar.activation(out=warm[:], in_=shift[:, 0:1], func=ACT.Exp, scale=0.0)
 
         grouped = keep.tile([P, PASSES, BATCH, PACK], BF16, align_bytes=64)
         h_codes = keep.tile([P, PASSES, BATCH], U32, align_bytes=64)

@@ -53,20 +53,19 @@ def tile_binarymlp_pb_kernel(tc, z2, g2, beta2, W3_words, W3_scales, b3, out):
         gain = keep.tile([P, PLANES], BF16)
         beta = keep.tile([P, PLANES], BF16)
 
+        nc.scalar.dma_start(
+            out=gain[:].rearrange("p (g t) -> p g t", t=PACK),
+            in_=g2.rearrange("(g p t) -> p g t", p=P, t=PACK),
+        )
+        nc.scalar.dma_start(
+            out=beta[:].rearrange("p (g t) -> p g t", t=PACK),
+            in_=beta2.rearrange("(g p t) -> p g t", p=P, t=PACK),
+        )
         z_sb = [keep.tile([P, B_TILES, K_PASS], BF16, name="z_sb_%d" % g) for g in range(PASSES)]
         for g in range(PASSES):
             for first in range(0, B_TILES, 2):
                 ks = slice(K_PASS * g, K_PASS * (g + 1))
                 nc.sync.dma_start(out=z_sb[g][:, first : first + 2, :], in_=z_rows[:, first : first + 2, ks])
-            if g == 0:
-                nc.sync.dma_start(
-                    out=gain[:].rearrange("p (g t) -> p g t", t=PACK),
-                    in_=g2.rearrange("(g p t) -> p g t", p=P, t=PACK),
-                )
-                nc.sync.dma_start(
-                    out=beta[:].rearrange("p (g t) -> p g t", t=PACK),
-                    in_=beta2.rearrange("(g p t) -> p g t", p=P, t=PACK),
-                )
 
         w_words = keep.tile([P, PASSES, 2 * CLASSES], U8, align_bytes=64)
         for g in range(PASSES):
@@ -95,9 +94,11 @@ def tile_binarymlp_pb_kernel(tc, z2, g2, beta2, W3_words, W3_scales, b3, out):
 
         stats = keep.tile([P, PAIRS, B_HALVES * STATS_PER_BANK, 6], F32)
         mean_var = keep.tile([P, PLANES, 2], F32)
-        neg_mean = keep.tile([P, PLANES], F32)
+        neg_mean_gain = keep.tile([P, PLANES], F32)
         gain_f32 = keep.tile([P, PLANES], F32)
+        neg_gain = keep.tile([P, PLANES], F32)
         nc.gpsimd.tensor_copy(out=gain_f32[:], in_=gain[:])
+        nc.gpsimd.tensor_scalar(out=neg_gain[:], in0=gain[:], scalar1=-1.0, scalar2=0.0, op0=ALU.mult, op1=ALU.add)
         rstd = keep.tile([P, PLANES], F32)
         scale = keep.tile([P, PLANES], F32)
         shift = keep.tile([P, PLANES], F32)
@@ -114,35 +115,49 @@ def tile_binarymlp_pb_kernel(tc, z2, g2, beta2, W3_words, W3_scales, b3, out):
                     )
             for e in range(2):
                 nc.vector.bn_aggr(out=mean_var[:, 2 * pair + e, :], in_=stats[:, pair, :, 3 * e : 3 * e + 3])
+
+        def reciprocal_deviation(pair):
+            js = slice(2 * pair, 2 * pair + 2)
             nc.scalar.activation(out=rstd[:, js], in_=mean_var[:, js, 1], func=ACT.Abs_reciprocal_sqrt, bias=BN_EPS, scale=1.0)
-            nc.scalar.activation(out=neg_mean[:, js], in_=mean_var[:, js, 0], func=ACT.Copy, scale=-1.0)
+            for j in range(2 * pair, 2 * pair + 2):
+                nc.scalar.activation(out=neg_mean_gain[:, j : j + 1], in_=mean_var[:, j, 0:1], func=ACT.Copy, scale=neg_gain[:, j : j + 1])
+
+        def scale_and_shift(pair):
             for j in range(2 * pair, 2 * pair + 2):
                 nc.scalar.activation(out=scale[:, j : j + 1], in_=rstd[:, j : j + 1], func=ACT.Copy, scale=gain_f32[:, j : j + 1])
-            for j in range(2 * pair, 2 * pair + 2):
                 nc.scalar.activation(
                     out=shift[:, j : j + 1],
-                    in_=scale[:, j : j + 1],
+                    in_=rstd[:, j : j + 1],
                     func=ACT.Identity,
                     bias=beta[:, j : j + 1],
-                    scale=neg_mean[:, j : j + 1],
+                    scale=neg_mean_gain[:, j : j + 1],
                 )
 
-        def norm_relu(pair):
-            for half in range(B_HALVES):
-                values = zT[(pair, half)][:].bitcast(BF16).rearrange("p (b e) -> p b e", e=2)
-                for e in range(2):
-                    j = 2 * pair + e
-                    nc.scalar.activation(
-                        out=planes[:, j // PACK, half, j % PACK, :],
-                        in_=values[:, :, e],
-                        func=ACT.Relu,
-                        bias=shift[:, j : j + 1],
-                        scale=scale[:, j : j + 1],
-                    )
+        def norm_relu(pair, half, e):
+            values = zT[(pair, half)][:].bitcast(BF16).rearrange("p (b e) -> p b e", e=2)
+            j = 2 * pair + e
+            nc.scalar.activation(
+                out=planes[:, j // PACK, half, j % PACK, :],
+                in_=values[:, :, e],
+                func=ACT.Relu,
+                bias=shift[:, j : j + 1],
+                scale=scale[:, j : j + 1],
+            )
 
+        statistics(0)
+        reciprocal_deviation(0)
+        scale_and_shift(0)
         for pair in range(PAIRS):
-            statistics(pair)
-            norm_relu(pair)
+            if pair + 1 < PAIRS:
+                statistics(pair + 1)
+            norm_relu(pair, 0, 0)
+            norm_relu(pair, 0, 1)
+            norm_relu(pair, 1, 0)
+            if pair + 1 < PAIRS:
+                reciprocal_deviation(pair + 1)
+            norm_relu(pair, 1, 1)
+            if pair + 1 < PAIRS:
+                scale_and_shift(pair + 1)
         warm = keep.tile([P, 1], F32)
         nc.scalar.activation(out=warm[:], in_=shift[:, 0:1], func=ACT.Exp, scale=0.0)
 

@@ -164,20 +164,29 @@ def tile_binarymlp_pb_kernel(tc, z2, g2, beta2, W3_words, W3_scales, b3, out):
         grouped = keep.tile([P, PASSES, BATCH, PACK], BF16, align_bytes=64)
         h_codes = keep.tile([P, PASSES, BATCH], U32, align_bytes=64)
         h_scales = keep.tile([P, PASSES, BATCH], U8, align_bytes=64)
-        for g in range(PASSES):
-            for half in range(B_HALVES):
-                bs = slice(BANK * half, BANK * (half + 1))
-                nc.vector.tensor_copy(
-                    out=grouped[:, g, bs, :].rearrange("p (c i) t -> p c t i", i=4),
-                    in_=planes[:, g, half, :, :].rearrange("p t (c i) -> p c t i", i=4),
-                )
-            for half in range(B_HALVES):
-                bs = slice(BANK * half, BANK * (half + 1))
-                nc.vector.quantize_mx(
-                    out=h_codes[:, g, bs].bitcast(FP8X4),
-                    scales=h_scales[:, g, bs],
-                    in_=grouped[:, g, bs, :].rearrange("p b t -> p (b t)"),
-                )
+        def regroup(g, half):
+            bs = slice(BANK * half, BANK * (half + 1))
+            nc.vector.tensor_copy(
+                out=grouped[:, g, bs, :].rearrange("p (c i) t -> p c t i", i=4),
+                in_=planes[:, g, half, :, :].rearrange("p t (c i) -> p c t i", i=4),
+            )
+
+        def quantise(g, half):
+            bs = slice(BANK * half, BANK * (half + 1))
+            nc.vector.quantize_mx(
+                out=h_codes[:, g, bs].bitcast(FP8X4),
+                scales=h_scales[:, g, bs],
+                in_=grouped[:, g, bs, :].rearrange("p b t -> p (b t)"),
+            )
+
+        regroup(0, 0)
+        regroup(0, 1)
+        quantise(0, 0)
+        quantise(0, 1)
+        regroup(1, 0)
+        quantise(1, 0)
+        regroup(1, 1)
+        quantise(1, 1)
 
         logits = keep.tile([P, B_TILES, CLASSES], F32)
         neg_max = keep.tile([P, B_TILES], F32)
@@ -249,12 +258,28 @@ def tile_binarymlp_pb_kernel(tc, z2, g2, beta2, W3_words, W3_scales, b3, out):
         add_bias(2)
         add_bias_beside_vector(3)
         matmuls(GROUP)
-        for i in range(GROUP):
-            max_and_exp_sum(i)
-        add_bias(GROUP)
+        max_and_exp_sum(0)
+        max_and_exp_sum(1)
+        add_bias_beside_vector(5)
+        max_and_exp_sum(2)
+        max_and_exp_sum(3)
+        add_bias(4)
         finish(0, nc.gpsimd)
-        for i in range(GROUP + 1, B_TILES):
-            add_bias(i)
-            max_and_exp_sum(i - 1)
-        max_and_exp_sum(B_TILES - 1)
-        finish(GROUP, nc.vector)
+        add_bias(6)
+        max_and_exp_sum(4)
+        max_and_exp_sum(5)
+        add_bias(7)
+        max_and_exp_sum(6)
+        max_and_exp_sum(7)
+        last = slice(GROUP, B_TILES)
+        nc.scalar.activation(out=log_sum[:, last], in_=exp_sum[:, last], func=ACT.Ln)
+        for i in range(GROUP, B_TILES):
+            nc.vector.tensor_scalar(
+                out=logits[:, i, :],
+                in0=logits[:, i, :],
+                scalar1=neg_max[:, i : i + 1],
+                scalar2=log_sum[:, i : i + 1],
+                op0=ALU.add,
+                op1=ALU.subtract,
+            )
+            nc.sync.dma_start(out=out_rows[:, i, :], in_=logits[:, i, :])

@@ -259,11 +259,11 @@ def tile_binarymlp_pb_kernel(tc, z2, g2, beta2, W3_words, W3_scales, b3, out):
         add_bias_beside_vector(3)
         matmuls(GROUP)
         max_and_exp_sum(0)
-        max_and_exp_sum(1)
-        add_bias_beside_vector(5)
         max_and_exp_sum(2)
-        max_and_exp_sum(3)
+        add_bias_beside_vector(5)
+        max_and_exp_sum(1)
         add_bias(4)
+        max_and_exp_sum(3)
         finish(0, nc.gpsimd)
         add_bias(6)
         max_and_exp_sum(4)

@@ -195,13 +195,12 @@ def tile_binarymlp_pb_kernel(tc, z2, g2, beta2, W3_words, W3_scales, b3, out):
 
         acc = {}
 
-        def matmuls(first):
-            tiles = range(first, first + TILES_PER_BANK)
-            for i in tiles:
+        def matmuls(first, order):
+            for i in range(first, first + TILES_PER_BANK):
                 for nh in range(N_HALVES):
                     acc[(i, nh)] = banks.tile([P, BANK], F32, tag="bank", name="acc_%d_%d" % (i, nh))
-            for g in range(PASSES):
-                for i in tiles:
+            for g, i in order:
+                if True:
                     for nh in range(N_HALVES):
                         nc.tensor.matmul_mx(
                             out=acc[(i, nh)][:],
@@ -252,21 +251,21 @@ def tile_binarymlp_pb_kernel(tc, z2, g2, beta2, W3_words, W3_scales, b3, out):
                 nc.scalar.copy(out=logits[:, i, ns], in_=acc[(i, nh)][:])
             nc.gpsimd.tensor_add(out=logits[:, i, :], in0=logits[:, i, :], in1=bias_rows[:])
 
-        matmuls(0)
-        add_bias(0)
+        matmuls(0, [(g, i) for g in range(PASSES) for i in range(GROUP)])
+        add_bias_beside_vector(0)
         add_bias_beside_vector(1)
         add_bias(2)
-        add_bias_beside_vector(3)
-        matmuls(GROUP)
-        max_and_exp_sum(0)
+        add_bias(3)
+        matmuls(GROUP, [(g, i) for i in range(GROUP, B_TILES) for g in range(PASSES)])
+        add_bias_beside_vector(4)
         max_and_exp_sum(2)
-        add_bias_beside_vector(5)
-        max_and_exp_sum(1)
-        add_bias(4)
         max_and_exp_sum(3)
+        max_and_exp_sum(0)
+        max_and_exp_sum(1)
         finish(0, nc.gpsimd)
-        add_bias(6)
+        add_bias(5)
         max_and_exp_sum(4)
+        add_bias(6)
         max_and_exp_sum(5)
         add_bias(7)
         max_and_exp_sum(6)

@@ -273,12 +273,16 @@ def tile_binarymlp_pb_kernel(tc, z2, g2, beta2, W3_words, W3_scales, b3, out):
         last = slice(GROUP, B_TILES)
         nc.scalar.activation(out=log_sum[:, last], in_=exp_sum[:, last], func=ACT.Ln)
         for i in range(GROUP, B_TILES):
-            nc.vector.tensor_scalar(
-                out=logits[:, i, :],
-                in0=logits[:, i, :],
-                scalar1=neg_max[:, i : i + 1],
-                scalar2=log_sum[:, i : i + 1],
-                op0=ALU.add,
-                op1=ALU.subtract,
-            )
-            nc.sync.dma_start(out=out_rows[:, i, :], in_=logits[:, i, :])
+            pieces = N_HALVES if i == GROUP else 1
+            width = CLASSES // pieces
+            for piece in range(pieces):
+                ns = slice(width * piece, width * (piece + 1))
+                nc.vector.tensor_scalar(
+                    out=logits[:, i, ns],
+                    in0=logits[:, i, ns],
+                    scalar1=neg_max[:, i : i + 1],
+                    scalar2=log_sum[:, i : i + 1],
+                    op0=ALU.add,
+                    op1=ALU.subtract,
+                )
+                nc.sync.dma_start(out=out_rows[:, i, ns], in_=logits[:, i, ns])

@@ -273,10 +273,10 @@ def tile_binarymlp_pb_kernel(tc, z2, g2, beta2, W3_words, W3_scales, b3, out):
         last = slice(GROUP, B_TILES)
         nc.scalar.activation(out=log_sum[:, last], in_=exp_sum[:, last], func=ACT.Ln)
         for i in range(GROUP, B_TILES):
-            pieces = N_HALVES if i == GROUP else 1
-            width = CLASSES // pieces
-            for piece in range(pieces):
-                ns = slice(width * piece, width * (piece + 1))
+            steps = 4 if i == GROUP else 1
+            width = CLASSES // steps
+            for step in range(steps):
+                ns = slice(width * step, width * (step + 1))
                 nc.vector.tensor_scalar(
                     out=logits[:, i, ns],
                     in0=logits[:, i, ns],
@@ -285,4 +285,9 @@ def tile_binarymlp_pb_kernel(tc, z2, g2, beta2, W3_words, W3_scales, b3, out):
                     op0=ALU.add,
                     op1=ALU.subtract,
                 )
-                nc.sync.dma_start(out=out_rows[:, i, ns], in_=logits[:, i, ns])
+                if steps > 1:
+                    nc.sync.dma_start(out=out_rows[:, i, ns], in_=logits[:, i, ns])
+            if steps == 1:
+                for nh in range(N_HALVES):
+                    ns = slice(BANK * nh, BANK * (nh + 1))
+                    nc.sync.dma_start(out=out_rows[:, i, ns], in_=logits[:, i, ns])

@@ -104,15 +104,14 @@ def tile_binarymlp_pb_kernel(tc, z2, g2, beta2, W3_words, W3_scales, b3, out):
         shift = keep.tile([P, PLANES], F32)
         planes = keep.tile([P, PASSES, B_HALVES, PACK, BANK], BF16)
 
-        def statistics(pair):
-            js = slice(2 * pair, 2 * pair + 2)
-            for half in range(B_HALVES):
-                values = zT[(pair, half)][:].bitcast(BF16)
-                for c in range(STATS_PER_BANK):
-                    nc.vector.bn_stats(
-                        out=stats[:, pair, STATS_PER_BANK * half + c, :],
-                        in_=values[:, STATS_MAX * c : STATS_MAX * (c + 1)],
-                    )
+        CHUNKS = B_HALVES * STATS_PER_BANK
+
+        def statistics(pair, chunk):
+            values = zT[(pair, chunk // STATS_PER_BANK)][:].bitcast(BF16)
+            c = chunk % STATS_PER_BANK
+            nc.vector.bn_stats(out=stats[:, pair, chunk, :], in_=values[:, STATS_MAX * c : STATS_MAX * (c + 1)])
+
+        def aggregate(pair):
             for e in range(2):
                 nc.vector.bn_aggr(out=mean_var[:, 2 * pair + e, :], in_=stats[:, pair, :, 3 * e : 3 * e + 3])
 
@@ -144,12 +143,19 @@ def tile_binarymlp_pb_kernel(tc, z2, g2, beta2, W3_words, W3_scales, b3, out):
                 scale=scale[:, j : j + 1],
             )
 
-        statistics(0)
+        for chunk in range(CHUNKS):
+            statistics(0, chunk)
+        statistics(1, 0)
+        aggregate(0)
         reciprocal_deviation(0)
         scale_and_shift(0)
         for pair in range(PAIRS):
             if pair + 1 < PAIRS:
-                statistics(pair + 1)
+                for chunk in range(1, CHUNKS):
+                    statistics(pair + 1, chunk)
+                if pair + 2 < PAIRS:
+                    statistics(pair + 2, 0)
+                aggregate(pair + 1)
             norm_relu(pair, 0, 0)
             norm_relu(pair, 0, 1)
             norm_relu(pair, 1, 0)
@@ -182,8 +188,8 @@ def tile_binarymlp_pb_kernel(tc, z2, g2, beta2, W3_words, W3_scales, b3, out):
         regroup(0, 0)
         regroup(0, 1)
         quantise(0, 0)
-        quantise(0, 1)
         regroup(1, 0)
+        quantise(0, 1)
         quantise(1, 0)
         regroup(1, 1)
         quantise(1, 1)

@@ -156,14 +156,24 @@ def tile_binarymlp_pb_kernel(tc, z2, g2, beta2, W3_words, W3_scales, b3, out):
                 if pair + 2 < PAIRS:
                     statistics(pair + 2, 0)
                 aggregate(pair + 1)
-            norm_relu(pair, 0, 0)
-            norm_relu(pair, 0, 1)
-            norm_relu(pair, 1, 0)
-            if pair + 1 < PAIRS:
+            if pair < 2:
+                norm_relu(pair, 0, 0)
+                norm_relu(pair, 0, 1)
+                norm_relu(pair, 1, 0)
                 reciprocal_deviation(pair + 1)
-            norm_relu(pair, 1, 1)
-            if pair + 1 < PAIRS:
+                norm_relu(pair, 1, 1)
                 scale_and_shift(pair + 1)
+            elif pair == 2:
+                norm_relu(2, 0, 0)
+                reciprocal_deviation(3)
+                norm_relu(2, 0, 1)
+                scale_and_shift(3)
+                norm_relu(3, 0, 0)
+                norm_relu(3, 0, 1)
+                norm_relu(2, 1, 0)
+                norm_relu(2, 1, 1)
+                norm_relu(3, 1, 0)
+                norm_relu(3, 1, 1)
         warm = keep.tile([P, 1], F32)
         nc.scalar.activation(out=warm[:], in_=shift[:, 0:1], func=ACT.Exp, scale=0.0)
 
@@ -257,7 +267,7 @@ def tile_binarymlp_pb_kernel(tc, z2, g2, beta2, W3_words, W3_scales, b3, out):
                 nc.scalar.copy(out=logits[:, i, ns], in_=acc[(i, nh)][:])
             nc.gpsimd.tensor_add(out=logits[:, i, :], in0=logits[:, i, :], in1=bias_rows[:])
 
-        matmuls(0, [(g, i) for g in range(PASSES) for i in range(GROUP)])
+        matmuls(0, [(0, 0), (0, 1), (0, 2), (1, 0), (1, 1), (1, 2), (0, 3), (1, 3)])
         add_bias_beside_vector(0)
         add_bias_beside_vector(1)
         add_bias(2)

@@ -143,6 +143,19 @@ def tile_binarymlp_pb_kernel(tc, z2, g2, beta2, W3_words, W3_scales, b3, out):
                 scale=scale[:, j : j + 1],
             )
 
+        grouped = keep.tile([P, PASSES, BATCH, PACK], BF16, align_bytes=64)
+
+        def regroup_gpsimd(g, half):
+            bs = slice(BANK * half, BANK * (half + 1))
+            nc.gpsimd.tensor_scalar(
+                out=grouped[:, g, bs, :],
+                in0=planes[:, g, half, :, :].rearrange("p t b -> p b t"),
+                scalar1=1.0,
+                scalar2=0.0,
+                op0=ALU.mult,
+                op1=ALU.add,
+            )
+
         for chunk in range(CHUNKS):
             statistics(0, chunk)
         statistics(1, 0)
@@ -159,14 +172,16 @@ def tile_binarymlp_pb_kernel(tc, z2, g2, beta2, W3_words, W3_scales, b3, out):
             if pair < 2:
                 norm_relu(pair, 0, 0)
                 norm_relu(pair, 0, 1)
+                if pair == 1:
+                    regroup_gpsimd(0, 0)
                 norm_relu(pair, 1, 0)
                 reciprocal_deviation(pair + 1)
                 norm_relu(pair, 1, 1)
                 scale_and_shift(pair + 1)
             elif pair == 2:
                 norm_relu(2, 0, 0)
-                reciprocal_deviation(3)
                 norm_relu(2, 0, 1)
+                reciprocal_deviation(3)
                 scale_and_shift(3)
                 norm_relu(3, 0, 0)
                 norm_relu(3, 0, 1)
@@ -177,7 +192,6 @@ def tile_binarymlp_pb_kernel(tc, z2, g2, beta2, W3_words, W3_scales, b3, out):
         warm = keep.tile([P, 1], F32)
         nc.scalar.activation(out=warm[:], in_=shift[:, 0:1], func=ACT.Exp, scale=0.0)
 
-        grouped = keep.tile([P, PASSES, BATCH, PACK], BF16, align_bytes=64)
         h_codes = keep.tile([P, PASSES, BATCH], U32, align_bytes=64)
         h_scales = keep.tile([P, PASSES, BATCH], U8, align_bytes=64)
         def regroup(g, half):
@@ -195,7 +209,6 @@ def tile_binarymlp_pb_kernel(tc, z2, g2, beta2, W3_words, W3_scales, b3, out):
                 in_=grouped[:, g, bs, :].rearrange("p b t -> p (b t)"),
             )
 
-        regroup(0, 0)
         regroup(0, 1)
         quantise(0, 0)
         regroup(1, 0)

@@ -83,14 +83,23 @@ def tile_binarymlp_pb_kernel(tc, z2, g2, beta2, W3_words, W3_scales, b3, out):
         nc.sync.dma_start(out=bias_rows[:], in_=b3.partition_broadcast(P))
 
         zT = {}
-        for g in range(PASSES):
+        z_bf16 = {}
+        for piece in range(B_TILES // 2):
+            bank = banks.tile([P, BANK], F32, tag="bank", name="zT_0_%d" % piece)
             for u in range(2):
-                for half in range(B_HALVES):
-                    bank = banks.tile([P, BANK], F32, tag="bank", name="zT_%d_%d_%d" % (g, u, half))
-                    zT[(2 * g + u, half)] = bank
-                    for slot in range(TILES_PER_BANK):
-                        words = z_sb[g][:, TILES_PER_BANK * half + slot, :].bitcast(F32)
-                        nc.tensor.transpose(bank[:, P * slot : P * (slot + 1)], words[:, u::2], identity[:])
+                for s in range(2):
+                    words = z_sb[0][:, 2 * piece + s, :].bitcast(F32)
+                    nc.tensor.transpose(bank[:, P * (2 * u + s) : P * (2 * u + s + 1)], words[:, u::2], identity[:])
+                z_bf16[(u, piece)] = bank[:].bitcast(BF16)[:, STATS_MAX * u : STATS_MAX * (u + 1)]
+        for u in range(2):
+            for half in range(B_HALVES):
+                bank = banks.tile([P, BANK], F32, tag="bank", name="zT_1_%d_%d" % (u, half))
+                zT[(2 + u, half)] = bank
+                for slot in range(TILES_PER_BANK):
+                    words = z_sb[1][:, TILES_PER_BANK * half + slot, :].bitcast(F32)
+                    nc.tensor.transpose(bank[:, P * slot : P * (slot + 1)], words[:, u::2], identity[:])
+                for c in range(STATS_PER_BANK):
+                    z_bf16[(2 + u, STATS_PER_BANK * half + c)] = bank[:].bitcast(BF16)[:, STATS_MAX * c : STATS_MAX * (c + 1)]
 
         stats = keep.tile([P, PAIRS, B_HALVES * STATS_PER_BANK, 6], F32)
         mean_var = keep.tile([P, PLANES, 2], F32)
@@ -107,9 +116,7 @@ def tile_binarymlp_pb_kernel(tc, z2, g2, beta2, W3_words, W3_scales, b3, out):
         CHUNKS = B_HALVES * STATS_PER_BANK
 
         def statistics(pair, chunk):
-            values = zT[(pair, chunk // STATS_PER_BANK)][:].bitcast(BF16)
-            c = chunk % STATS_PER_BANK
-            nc.vector.bn_stats(out=stats[:, pair, chunk, :], in_=values[:, STATS_MAX * c : STATS_MAX * (c + 1)])
+            nc.vector.bn_stats(out=stats[:, pair, chunk, :], in_=z_bf16[(pair, chunk)])
 
         def aggregate(pair):
             for e in range(2):
@@ -143,6 +150,18 @@ def tile_binarymlp_pb_kernel(tc, z2, g2, beta2, W3_words, W3_scales, b3, out):
                 scale=scale[:, j : j + 1],
             )
 
+        def norm_relu_chunk(pair, chunk, e):
+            j = 2 * pair + e
+            width = STATS_MAX // 2
+            first = width * (chunk % STATS_PER_BANK)
+            nc.scalar.activation(
+                out=planes[:, j // PACK, chunk // STATS_PER_BANK, j % PACK, first : first + width],
+                in_=z_bf16[(pair, chunk)].rearrange("p (b e) -> p b e", e=2)[:, :, e],
+                func=ACT.Relu,
+                bias=shift[:, j : j + 1],
+                scale=scale[:, j : j + 1],
+            )
+
         grouped = keep.tile([P, PASSES, BATCH, PACK], BF16, align_bytes=64)
 
         def regroup_gpsimd(g, half):
@@ -170,13 +189,16 @@ def tile_binarymlp_pb_kernel(tc, z2, g2, beta2, W3_words, W3_scales, b3, out):
                     statistics(pair + 2, 0)
                 aggregate(pair + 1)
             if pair < 2:
-                norm_relu(pair, 0, 0)
-                norm_relu(pair, 0, 1)
+                for chunk in range(2):
+                    norm_relu_chunk(pair, chunk, 0)
+                    norm_relu_chunk(pair, chunk, 1)
                 if pair == 1:
                     regroup_gpsimd(0, 0)
-                norm_relu(pair, 1, 0)
+                norm_relu_chunk(pair, 2, 0)
+                norm_relu_chunk(pair, 2, 1)
+                norm_relu_chunk(pair, 3, 0)
                 reciprocal_deviation(pair + 1)
-                norm_relu(pair, 1, 1)
+                norm_relu_chunk(pair, 3, 1)
                 scale_and_shift(pair + 1)
             elif pair == 2:
                 norm_relu(2, 0, 0)

from contextlib import ExitStack

import concourse.mybir as mybir
from concourse.masks import make_identity

F32 = mybir.dt.float32
BF16 = mybir.dt.bfloat16
U8 = mybir.dt.uint8
U32 = mybir.dt.uint32
I32 = mybir.dt.int32
FP8X4 = mybir.dt.float8_e4m3fn_x4
FP4X4 = mybir.dt.float4_e2m1fn_x4
ALU = mybir.AluOpType
ACT = mybir.ActivationFunctionType
AXIS = mybir.AxisListType

P = 128
PACK = 4
K_PASS = P * PACK
BATCH = 1024
FEATURES = 1024
CLASSES = 1024
PASSES = FEATURES // K_PASS
PLANES = PASSES * PACK
PAIRS = PLANES // 2
B_TILES = BATCH // P
BANK = 512
B_HALVES = BATCH // BANK
TILES_PER_BANK = BANK // P
N_HALVES = CLASSES // BANK
STATS_MAX = 512
STATS_PER_BANK = 2 * BANK // STATS_MAX
GROUP = 4
BN_EPS = 1e-5

FLOPS = 2 * BATCH * FEATURES * CLASSES


def tile_binarymlp_pb_kernel(tc, z2, g2, beta2, W3_words, W3_scales, b3, out):
    nc = tc.nc
    with ExitStack() as ctx:
        ctx.enter_context(tc.manual_schedule())
        keep = ctx.enter_context(tc.tile_pool(name="keep", bufs=1))
        scratch = ctx.enter_context(tc.tile_pool(name="scratch", bufs=2))
        banks = ctx.enter_context(tc.psum_pool(name="banks", bufs=8))

        identity = keep.tile([P, P], F32)
        make_identity(nc, identity[:])

        z_rows = z2.rearrange("(p i) k -> p i k", i=B_TILES)
        out_rows = out.rearrange("(p i) n -> p i n", i=B_TILES)

        gain = keep.tile([P, PLANES], BF16)
        beta = keep.tile([P, PLANES], BF16)

        nc.scalar.dma_start(
            out=gain[:].rearrange("p (g t) -> p g t", t=PACK),
            in_=g2.rearrange("(g p t) -> p g t", p=P, t=PACK),
        )
        nc.scalar.dma_start(
            out=beta[:].rearrange("p (g t) -> p g t", t=PACK),
            in_=beta2.rearrange("(g p t) -> p g t", p=P, t=PACK),
        )
        z_sb = [keep.tile([P, B_TILES, K_PASS], BF16, name="z_sb_%d" % g) for g in range(PASSES)]
        for g in range(PASSES):
            for first in range(0, B_TILES, 2):
                ks = slice(K_PASS * g, K_PASS * (g + 1))
                nc.sync.dma_start(out=z_sb[g][:, first : first + 2, :], in_=z_rows[:, first : first + 2, ks])

        w_words = keep.tile([P, PASSES, 2 * CLASSES], U8, align_bytes=64)
        for g in range(PASSES):
            nc.sync.dma_start(out=w_words[:, g, :].bitcast(I32), in_=W3_words[g].bitcast(I32))

        w_scales = keep.tile([P, PASSES, CLASSES], U8, align_bytes=64)
        nc.vector.memset(w_scales[:].bitcast(I32), 0)
        for quadrant in range(4):
            nc.sync.dma_start(
                out=w_scales[32 * quadrant : 32 * quadrant + 4, :, :].bitcast(I32),
                in_=W3_scales[:, 4 * quadrant : 4 * quadrant + 4, :].rearrange("g r n -> r g n").bitcast(I32),
            )

        bias_rows = keep.tile([P, CLASSES], BF16)
        nc.sync.dma_start(out=bias_rows[:], in_=b3.partition_broadcast(P))

        zT = {}
        z_bf16 = {}
        for piece in range(B_TILES // 2):
            bank = banks.tile([P, BANK], F32, tag="bank", name="zT_0_%d" % piece)
            for u in range(2):
                for s in range(2):
                    words = z_sb[0][:, 2 * piece + s, :].bitcast(F32)
                    nc.tensor.transpose(bank[:, P * (2 * u + s) : P * (2 * u + s + 1)], words[:, u::2], identity[:])
                z_bf16[(u, piece)] = bank[:].bitcast(BF16)[:, STATS_MAX * u : STATS_MAX * (u + 1)]
        for u in range(2):
            for half in range(B_HALVES):
                bank = banks.tile([P, BANK], F32, tag="bank", name="zT_1_%d_%d" % (u, half))
                zT[(2 + u, half)] = bank
                for slot in range(TILES_PER_BANK):
                    words = z_sb[1][:, TILES_PER_BANK * half + slot, :].bitcast(F32)
                    nc.tensor.transpose(bank[:, P * slot : P * (slot + 1)], words[:, u::2], identity[:])
                for c in range(STATS_PER_BANK):
                    z_bf16[(2 + u, STATS_PER_BANK * half + c)] = bank[:].bitcast(BF16)[:, STATS_MAX * c : STATS_MAX * (c + 1)]

        stats = keep.tile([P, PAIRS, B_HALVES * STATS_PER_BANK, 6], F32)
        mean_var = keep.tile([P, PLANES, 2], F32)
        neg_mean_gain = keep.tile([P, PLANES], F32)
        gain_f32 = keep.tile([P, PLANES], F32)
        neg_gain = keep.tile([P, PLANES], F32)
        nc.gpsimd.tensor_copy(out=gain_f32[:], in_=gain[:])
        nc.gpsimd.tensor_scalar(out=neg_gain[:], in0=gain[:], scalar1=-1.0, scalar2=0.0, op0=ALU.mult, op1=ALU.add)
        rstd = keep.tile([P, PLANES], F32)
        scale = keep.tile([P, PLANES], F32)
        shift = keep.tile([P, PLANES], F32)
        planes = keep.tile([P, PASSES, B_HALVES, PACK, BANK], BF16)

        CHUNKS = B_HALVES * STATS_PER_BANK

        def statistics(pair, chunk):
            nc.vector.bn_stats(out=stats[:, pair, chunk, :], in_=z_bf16[(pair, chunk)])

        def aggregate(pair):
            for e in range(2):
                nc.vector.bn_aggr(out=mean_var[:, 2 * pair + e, :], in_=stats[:, pair, :, 3 * e : 3 * e + 3])

        def reciprocal_deviation(pair):
            js = slice(2 * pair, 2 * pair + 2)
            nc.scalar.activation(out=rstd[:, js], in_=mean_var[:, js, 1], func=ACT.Abs_reciprocal_sqrt, bias=BN_EPS, scale=1.0)
            for j in range(2 * pair, 2 * pair + 2):
                nc.scalar.activation(out=neg_mean_gain[:, j : j + 1], in_=mean_var[:, j, 0:1], func=ACT.Copy, scale=neg_gain[:, j : j + 1])

        def scale_and_shift(pair):
            for j in range(2 * pair, 2 * pair + 2):
                nc.scalar.activation(out=scale[:, j : j + 1], in_=rstd[:, j : j + 1], func=ACT.Copy, scale=gain_f32[:, j : j + 1])
                nc.scalar.activation(
                    out=shift[:, j : j + 1],
                    in_=rstd[:, j : j + 1],
                    func=ACT.Identity,
                    bias=beta[:, j : j + 1],
                    scale=neg_mean_gain[:, j : j + 1],
                )

        def norm_relu(pair, half, e):
            values = zT[(pair, half)][:].bitcast(BF16).rearrange("p (b e) -> p b e", e=2)
            j = 2 * pair + e
            nc.scalar.activation(
                out=planes[:, j // PACK, half, j % PACK, :],
                in_=values[:, :, e],
                func=ACT.Relu,
                bias=shift[:, j : j + 1],
                scale=scale[:, j : j + 1],
            )

        def norm_relu_chunk(pair, chunk, e):
            j = 2 * pair + e
            width = STATS_MAX // 2
            first = width * (chunk % STATS_PER_BANK)
            nc.scalar.activation(
                out=planes[:, j // PACK, chunk // STATS_PER_BANK, j % PACK, first : first + width],
                in_=z_bf16[(pair, chunk)].rearrange("p (b e) -> p b e", e=2)[:, :, e],
                func=ACT.Relu,
                bias=shift[:, j : j + 1],
                scale=scale[:, j : j + 1],
            )

        grouped = keep.tile([P, PASSES, BATCH, PACK], BF16, align_bytes=64)

        def regroup_gpsimd(g, half):
            bs = slice(BANK * half, BANK * (half + 1))
            nc.gpsimd.tensor_scalar(
                out=grouped[:, g, bs, :],
                in0=planes[:, g, half, :, :].rearrange("p t b -> p b t"),
                scalar1=1.0,
                scalar2=0.0,
                op0=ALU.mult,
                op1=ALU.add,
            )

        for chunk in range(CHUNKS):
            statistics(0, chunk)
        statistics(1, 0)
        aggregate(0)
        reciprocal_deviation(0)
        scale_and_shift(0)
        for pair in range(PAIRS):
            if pair + 1 < PAIRS:
                for chunk in range(1, CHUNKS):
                    statistics(pair + 1, chunk)
                if pair + 2 < PAIRS:
                    statistics(pair + 2, 0)
                aggregate(pair + 1)
            if pair < 2:
                for chunk in range(2):
                    norm_relu_chunk(pair, chunk, 0)
                    norm_relu_chunk(pair, chunk, 1)
                if pair == 1:
                    regroup_gpsimd(0, 0)
                norm_relu_chunk(pair, 2, 0)
                norm_relu_chunk(pair, 2, 1)
                norm_relu_chunk(pair, 3, 0)
                reciprocal_deviation(pair + 1)
                norm_relu_chunk(pair, 3, 1)
                scale_and_shift(pair + 1)
            elif pair == 2:
                norm_relu(2, 0, 0)
                norm_relu(2, 0, 1)
                reciprocal_deviation(3)
                scale_and_shift(3)
                norm_relu(3, 0, 0)
                norm_relu(3, 0, 1)
                norm_relu(2, 1, 0)
                norm_relu(2, 1, 1)
                norm_relu(3, 1, 0)
                norm_relu(3, 1, 1)
        warm = keep.tile([P, 1], F32)
        nc.scalar.activation(out=warm[:], in_=shift[:, 0:1], func=ACT.Exp, scale=0.0)

        h_codes = keep.tile([P, PASSES, BATCH], U32, align_bytes=64)
        h_scales = keep.tile([P, PASSES, BATCH], U8, align_bytes=64)
        def regroup(g, half):
            bs = slice(BANK * half, BANK * (half + 1))
            nc.vector.tensor_copy(
                out=grouped[:, g, bs, :].rearrange("p (c i) t -> p c t i", i=4),
                in_=planes[:, g, half, :, :].rearrange("p t (c i) -> p c t i", i=4),
            )

        def quantise(g, half):
            bs = slice(BANK * half, BANK * (half + 1))
            nc.vector.quantize_mx(
                out=h_codes[:, g, bs].bitcast(FP8X4),
                scales=h_scales[:, g, bs],
                in_=grouped[:, g, bs, :].rearrange("p b t -> p (b t)"),
            )

        regroup(0, 1)
        quantise(0, 0)
        regroup(1, 0)
        quantise(0, 1)
        quantise(1, 0)
        regroup(1, 1)
        quantise(1, 1)

        logits = keep.tile([P, B_TILES, CLASSES], F32)
        neg_max = keep.tile([P, B_TILES], F32)
        exp_sum = keep.tile([P, B_TILES], F32)
        log_sum = keep.tile([P, B_TILES], F32)

        acc = {}

        def matmuls(first, order):
            for i in range(first, first + TILES_PER_BANK):
                for nh in range(N_HALVES):
                    acc[(i, nh)] = banks.tile([P, BANK], F32, tag="bank", name="acc_%d_%d" % (i, nh))
            for g, i in order:
                if True:
                    for nh in range(N_HALVES):
                        nc.tensor.matmul_mx(
                            out=acc[(i, nh)][:],
                            lhsT=h_codes[:, g, P * i : P * (i + 1)].bitcast(FP8X4),
                            lhsT_scale=h_scales[:, g, P * i : P * (i + 1)],
                            rhs=w_words[:, g, 2 * BANK * nh : 2 * BANK * (nh + 1)].bitcast(FP4X4),
                            rhs_scale=w_scales[:, g, BANK * nh : BANK * (nh + 1)],
                            start=(g == 0),
                            stop=(g == PASSES - 1),
                        )

        def add_bias(i):
            for nh in range(N_HALVES):
                ns = slice(BANK * nh, BANK * (nh + 1))
                nc.vector.tensor_add(out=logits[:, i, ns], in0=acc[(i, nh)][:], in1=bias_rows[:, ns])

        def max_and_exp_sum(i):
            nc.vector.tensor_reduce(out=neg_max[:, i : i + 1], in_=logits[:, i, :], axis=AXIS.X, op=ALU.max, negate=True)
            exps = scratch.tile([P, CLASSES], BF16)
            nc.scalar.activation(
                out=exps[:],
                in_=logits[:, i, :],
                func=ACT.Exp,
                bias=neg_max[:, i : i + 1],
                scale=1.0,
                accum_out=exp_sum[:, i : i + 1],
            )

        def finish(first, engine):
            group = slice(first, first + GROUP)
            nc.scalar.activation(out=log_sum[:, group], in_=exp_sum[:, group], func=ACT.Ln)
            neg_lse = keep.tile([P, GROUP], F32, name="neg_lse_%d" % first)
            engine.tensor_sub(out=neg_lse[:], in0=neg_max[:, group], in1=log_sum[:, group])
            for i in range(first, first + GROUP):
                engine.tensor_scalar(
                    out=logits[:, i, :],
                    in0=logits[:, i, :],
                    scalar1=1.0,
                    scalar2=neg_lse[:, i - first : i - first + 1],
                    op0=ALU.mult,
                    op1=ALU.add,
                )
                nc.sync.dma_start(out=out_rows[:, i, :], in_=logits[:, i, :])

        def add_bias_beside_vector(i):
            for nh in range(N_HALVES):
                ns = slice(BANK * nh, BANK * (nh + 1))
                nc.scalar.copy(out=logits[:, i, ns], in_=acc[(i, nh)][:])
            nc.gpsimd.tensor_add(out=logits[:, i, :], in0=logits[:, i, :], in1=bias_rows[:])

        matmuls(0, [(0, 0), (0, 1), (0, 2), (1, 0), (1, 1), (1, 2), (0, 3), (1, 3)])
        add_bias_beside_vector(0)
        add_bias_beside_vector(1)
        add_bias(2)
        add_bias(3)
        matmuls(GROUP, [(g, i) for i in range(GROUP, B_TILES) for g in range(PASSES)])
        add_bias_beside_vector(4)
        max_and_exp_sum(2)
        max_and_exp_sum(3)
        max_and_exp_sum(0)
        max_and_exp_sum(1)
        finish(0, nc.gpsimd)
        add_bias(5)
        max_and_exp_sum(4)
        add_bias(6)
        max_and_exp_sum(5)
        add_bias(7)
        max_and_exp_sum(6)
        max_and_exp_sum(7)
        last = slice(GROUP, B_TILES)
        nc.scalar.activation(out=log_sum[:, last], in_=exp_sum[:, last], func=ACT.Ln)
        for i in range(GROUP, B_TILES):
            steps = 4 if i == GROUP else 1
            width = CLASSES // steps
            for step in range(steps):
                ns = slice(width * step, width * (step + 1))
                nc.vector.tensor_scalar(
                    out=logits[:, i, ns],
                    in0=logits[:, i, ns],
                    scalar1=neg_max[:, i : i + 1],
                    scalar2=log_sum[:, i : i + 1],
                    op0=ALU.add,
                    op1=ALU.subtract,
                )
                if steps > 1:
                    nc.sync.dma_start(out=out_rows[:, i, ns], in_=logits[:, i, ns])
            if steps == 1:
                for nh in range(N_HALVES):
                    ns = slice(BANK * nh, BANK * (nh + 1))
                    nc.sync.dma_start(out=out_rows[:, i, ns], in_=logits[:, i, ns])
